import numpy as np
import ml_dtypes


def mxq(x, axis, fmt="e4m3"):
    dtype, down = {"e4m3": (ml_dtypes.float8_e4m3fn, 7), "e5m2": (ml_dtypes.float8_e5m2, 14)}[fmt]
    v = np.moveaxis(np.asarray(x, np.float32).astype(ml_dtypes.bfloat16).astype(np.float64), axis, -1)
    blocks = v.reshape(v.shape[:-1] + (-1, 32))
    amax = np.abs(blocks).max(-1, keepdims=True)
    byte = np.maximum(np.where(amax > 0, np.frexp(amax)[1] - 1 + 127, 0) - down, 1)
    scale = np.exp2(byte - 127.0)
    codes = (blocks / scale).astype(np.float32).astype(dtype).astype(np.float64)
    return np.moveaxis((codes * scale).reshape(v.shape), -1, axis)


WIDE = False


def mx_kscale(k):
    if not WIDE:
        return np.ones(k)
    levels = np.array([10, -10, 5, -5, 0])
    a = np.random.permutation(np.resize(levels, k // 512 * 4)).reshape(k // 512, 4)
    idx = np.arange(k)
    return np.exp2(a[idx // 512, idx % 128 // 32])


BF16 = ml_dtypes.bfloat16


def bf(x):
    return np.asarray(x, np.float32).astype(BF16)


def f64(x):
    return np.asarray(x).astype(np.float64)


B, S, D, O = 2, 256, 2048, 4096

EPS = 1.0 / 137.0


def setup_inputs():
    s = mx_kscale(D)
    p = np.exp2(np.round(0.5 * np.log2(np.mean(1.0 / (s * s)))))
    q = np.exp2(np.round(0.5 * np.log2(np.mean(s * s))))
    return {"x": bf(np.random.standard_normal((B, S, D)) * 0.5 * s * p),
            "kernel": bf(np.random.standard_normal((D, O)) * 0.5 / s[:, None] * q),
            "bias": bf(np.random.standard_normal(O) * 0.1),
            "alpha": bf(1.0 + 0.1 * np.random.standard_normal(1))}


def reference(x, kernel, bias, alpha):
    xf, kf = f64(x), f64(kernel)
    y = mxq(xf, 2, "e4m3") @ mxq(kf, 0, "e4m3")
    x_sq = np.sum(xf * xf, axis=-1, keepdims=True)
    k_sq = np.sum(kf * kf, axis=0, keepdims=True)
    distances = x_sq + k_sq - 2.0 * y
    y = (y * y) / (distances + EPS)
    y = y + f64(bias).reshape((1,) * (y.ndim - 1) + (-1,))
    scale = (np.sqrt(float(O)) / np.log1p(float(O))) ** f64(alpha)
    return y * scale

@@ -1,0 +1,238 @@
+from contextlib import ExitStack
+
+import concourse.mybir as mybir
+from concourse.masks import make_identity
+
+F32 = mybir.dt.float32
+BF16 = mybir.dt.bfloat16
+U32 = mybir.dt.uint32
+U8 = mybir.dt.uint8
+FP8X4 = mybir.dt.float8_e4m3fn_x4
+ALU = mybir.AluOpType
+ACT = mybir.ActivationFunctionType
+AX = mybir.AxisListType
+
+P = 128
+D = 2048
+O = 4096
+T = 512
+MT = T // P
+PACK = 4
+K_PASS = P * PACK
+PASSES = D // K_PASS
+CH = 512
+NCH = O // CH
+BLK = 128
+NBLK = CH // BLK
+ROWS = PASSES * PACK
+EPS = 1.0 / 137.0
+LN_C0 = 2.0404600064606253
+
+FLOPS = 2 * T * D * O
+
+GRAM = [2,1,1,1,1,1,1,2]
+GP_ADD = [[],[],[],[],[],[],[],[]]
+X_EVAC_V = 4
+CB_V = []
+AHEAD = 3
+MANUAL = False
+
+
+def tile_yatnmn_kernel(tc, x, kernel, bias, alpha, out):
+    nc = tc.nc
+    xf = x.flatten_outer_dims()
+    of = out.flatten_outer_dims()
+
+    with ExitStack() as ctx:
+        if MANUAL:
+            ctx.enter_context(tc.manual_schedule())
+        const = ctx.enter_context(tc.tile_pool(name="const", bufs=1))
+        rawp = ctx.enter_context(tc.tile_pool(name="rawp", bufs=4))
+        grp = ctx.enter_context(tc.tile_pool(name="grp", bufs=2))
+        codep = ctx.enter_context(tc.tile_pool(name="codep", bufs=3))
+        smallp = ctx.enter_context(tc.tile_pool(name="smallp", bufs=3))
+        workp = ctx.enter_context(tc.tile_pool(name="workp", bufs=8))
+        psy = ctx.enter_context(tc.psum_pool(name="psy", bufs=4))
+        pstr = ctx.enter_context(tc.psum_pool(name="pstr", bufs=2))
+        psg = ctx.enter_context(tc.psum_pool(name="psg", bufs=1))
+        psb = ctx.enter_context(tc.psum_pool(name="psb", bufs=1))
+
+        ident_b = const.tile([P, P], BF16)
+        make_identity(nc, ident_b[:])
+        ident_f = const.tile([P, P], F32)
+        make_identity(nc, ident_f[:])
+
+        raws = {}
+        codes = {}
+        cbs = {}
+
+        def load_pass(n, c):
+            nc.sync.dma_start(
+                out=raws[n][:, c, :, :],
+                in_=kernel[c * K_PASS:(c + 1) * K_PASS, n * CH:(n + 1) * CH].rearrange(
+                    "(p j) w -> p j w", j=PACK))
+
+        def load(n):
+            raw = rawp.tile([P, PASSES, PACK, CH], BF16, tag="raw")
+            raws[n] = raw
+            for c in range(PASSES):
+                load_pass(n, c)
+
+        def quant(n):
+            raw = raws[n]
+            gk = grp.tile([P, PASSES, PACK * CH], BF16, tag="gk", align_bytes=64)
+            kc = codep.tile([P, PASSES, CH], U32, align_bytes=64)
+            ksc = codep.tile([P, PASSES, CH], U8, align_bytes=64)
+            codes[n] = (kc, ksc)
+
+            def regroup(c):
+                nc.vector.tensor_copy(
+                    out=gk[:, c, :].rearrange("p (q i t) -> p q t i", i=4, t=PACK),
+                    in_=raw[:, c, :, :].rearrange("p t (q i) -> p q t i", i=4))
+
+            def quantise(c):
+                nc.vector.quantize_mx(out=kc[:, c, :].bitcast(FP8X4), scales=ksc[:, c, :],
+                                      in_=gk[:, c, :])
+
+            regroup(0)
+            for c in range(1, PASSES):
+                regroup(c)
+                quantise(c - 1)
+            quantise(PASSES - 1)
+
+        def ksq_chunk(n):
+            raw = raws[n]
+            ng = GRAM[n]
+            ksq = smallp.tile([P, NBLK], F32)
+            part = smallp.tile([P, 2 * NBLK], F32)
+            gram = psg.tile([P, NBLK, P], F32)
+            for b in range(ng):
+                for r in range(ROWS):
+                    c, j = divmod(r, PACK)
+                    nc.tensor.matmul(out=gram[:, b, :], lhsT=raw[:, c, j, b * BLK:(b + 1) * BLK],
+                                     rhs=raw[:, c, j, b * BLK:(b + 1) * BLK],
+                                     start=(r == 0), stop=(r == ROWS - 1))
+            for b in range(ng, NBLK):
+                for h in range(2):
+                    tr = pstr.tile([P, 8 * P], BF16)
+                    for i in range(8):
+                        c, j = divmod(h * 8 + i, PACK)
+                        nc.tensor.transpose(out=tr[:, i * P:(i + 1) * P],
+                                            in_=raw[:, c, j, b * BLK:(b + 1) * BLK],
+                                            identity=ident_b[:])
+                    idx = b * 2 + h
+                    nc.scalar.activation(out=junk[:, 0:8 * P], in_=tr[:], func=ACT.Square,
+                                         accum_out=part[:, idx:idx + 1])
+            for b in range(ng):
+                nc.vector.scalar_tensor_tensor(out=junkf[:], in0=gram[:, b, :], scalar=1.0, in1=ident_f[:],
+                                               op0=ALU.mult, op1=ALU.mult, accum_out=ksq[:, b:b + 1])
+            nc.vector.tensor_reduce(out=ksq[:, ng:NBLK],
+                                    in_=part[:, 2 * ng:2 * NBLK].rearrange("p (b h) -> p b h", h=2),
+                                    axis=AX.X, op=ALU.add)
+            bc = psb.tile([P, CH], F32)
+            for b in range(NBLK):
+                nc.tensor.matmul(out=bc[:, b * BLK:(b + 1) * BLK],
+                                 lhsT=ksq[:, b:b + 1].to_broadcast([P, P]), rhs=ident_f[:],
+                                 start=True, stop=True)
+            cb = smallp.tile([P, CH], F32)
+            cbs[n] = cb
+            if n in CB_V:
+                nc.vector.tensor_scalar(out=cb[:], in0=bc[:], scalar1=0.5, scalar2=0.5 * EPS,
+                                        op0=ALU.mult, op1=ALU.add)
+            else:
+                nc.scalar.activation(out=cb[:], in_=bc[:], func=ACT.Copy, scale=0.5, bias=0.5 * EPS)
+
+        def mx_epilogue(n):
+            cols = slice(n * CH, (n + 1) * CH)
+            kc, ksc = codes[n]
+            cb = cbs[n]
+            for mt in range(MT):
+                y = psy.tile([P, CH], F32, tag="y")
+                for c in range(PASSES):
+                    nc.tensor.matmul_mx(
+                        out=y[:],
+                        lhsT=xc[:, c, mt * P:(mt + 1) * P].bitcast(FP8X4),
+                        lhsT_scale=xsc[:, c, mt * P:(mt + 1) * P],
+                        rhs=kc[:, c, :].bitcast(FP8X4),
+                        rhs_scale=ksc[:, c, :],
+                        start=(c == 0), stop=(c == PASSES - 1))
+                w = workp.tile([P, CH], F32)
+                nc.vector.scalar_tensor_tensor(out=w[:], in0=y[:], scalar=xhalf[:, mt:mt + 1], in1=cb[:],
+                                               op0=ALU.subtract, op1=ALU.subtract)
+                nc.scalar.activation(out=w[:], in_=w[:], func=ACT.Abs_reciprocal_sqrt, scale=2.0)
+                nc.vector.tensor_tensor(out=w[:], in0=y[:], in1=w[:], op=ALU.mult)
+                nc.scalar.activation(out=w[:], in_=w[:], func=ACT.Square, scale=sqs[:, 0:1])
+                if mt in GP_ADD[n]:
+                    nc.gpsimd.tensor_tensor(out=w[:], in0=w[:], in1=bs[:, cols], op=ALU.add)
+                else:
+                    nc.vector.scalar_tensor_tensor(out=w[:], in0=bias_b[:, cols], scalar=sfac[:, 0:1],
+                                                   in1=w[:], op0=ALU.mult, op1=ALU.add)
+                if n == NCH - 1:
+                    nc.sync.dma_start(out=of[mt * P:(mt + 1) * P, cols], in_=w[:])
+                else:
+                    nc.gpsimd.dma_start(out=of[mt * P:(mt + 1) * P, cols], in_=w[:])
+
+        al = const.tile([P, 1], BF16)
+        nc.scalar.dma_start(out=al[:], in_=alpha.partition_broadcast(P))
+        raw0 = rawp.tile([P, PASSES, PACK, CH], BF16, tag="raw")
+        raws[0] = raw0
+        x_sb = rawp.tile([P, MT, D], BF16, tag="raw")
+        for i in range(MT):
+            load_pass(0, i)
+            nc.sync.dma_start(out=x_sb[:, i, :], in_=xf[i * P:(i + 1) * P, :])
+        bias_b = const.tile([P, O], BF16)
+        nc.sync.dma_start(out=bias_b[:], in_=bias.partition_broadcast(P))
+        for n in range(1, AHEAD):
+            load(n)
+
+        sqs = const.tile([P, 1], F32)
+        nc.scalar.activation(out=sqs[:], in_=al[:], func=ACT.Exp, scale=0.5 * LN_C0)
+        sfac = const.tile([P, 1], F32)
+        nc.scalar.activation(out=sfac[:], in_=al[:], func=ACT.Exp, scale=LN_C0)
+        junk = const.tile([P, D], BF16)
+        junkf = const.tile([P, P], F32)
+        if any(len(g) > 0 for g in GP_ADD):
+            bs = const.tile([P, O], F32)
+            nc.gpsimd.tensor_scalar(out=bs[:], in0=bias_b[:], scalar1=sfac[:, 0:1], scalar2=0.0,
+                                    op0=ALU.mult, op1=ALU.add)
+
+        quant(0)
+
+        xw = x_sb[:].bitcast(F32).rearrange("p m (c q u) -> p m c q u", c=PASSES, q=P, u=2)
+        gx = grp.tile([P, PASSES, PACK * T], BF16, tag="gk", align_bytes=64)
+        gx32 = gx[:].bitcast(F32).rearrange("p c (t u) -> p c t u", u=2)
+        xc = const.tile([P, PASSES, T], U32, align_bytes=64)
+        xsc = const.tile([P, PASSES, T], U8, align_bytes=64)
+        for c in range(PASSES):
+            for half in range(2):
+                xt = psy.tile([P, 2, 2 * P], F32, tag="y")
+                for u in range(2):
+                    for ml in range(2):
+                        nc.tensor.transpose(out=xt[:, u, ml * P:(ml + 1) * P],
+                                            in_=xw[:, 2 * half + ml, c, :, u],
+                                            identity=ident_f[:])
+                dst = gx32[:, c, half * 2 * P:(half + 1) * 2 * P, :]
+                src = xt[:].rearrange("p u t -> p t u")
+                if c * 2 + half < X_EVAC_V:
+                    nc.vector.tensor_copy(out=dst, in_=src)
+                else:
+                    nc.scalar.copy(out=dst, in_=src)
+        for c in range(PASSES):
+            nc.vector.quantize_mx(out=xc[:, c, :].bitcast(FP8X4), scales=xsc[:, c, :], in_=gx[:, c, :])
+
+        ksq_chunk(0)
+
+        xs_raw = const.tile([P, MT], F32)
+        for mt in range(MT):
+            nc.scalar.activation(out=junk[:], in_=x_sb[:, mt, :], func=ACT.Square,
+                                 accum_out=xs_raw[:, mt:mt + 1])
+        xhalf = const.tile([P, MT], F32)
+        nc.vector.tensor_scalar(out=xhalf[:], in0=xs_raw[:], scalar1=0.5, scalar2=None, op0=ALU.mult)
+
+        for n in range(NCH):
+            if n + AHEAD < NCH:
+                load(n + AHEAD)
+            if n + 1 < NCH:
+                quant(n + 1)
+                ksq_chunk(n + 1)
+            mx_epilogue(n)

@@ -31,7 +31,7 @@ LN_C0 = 2.0404600064606253
 FLOPS = 2 * T * D * O
 
 GRAM = [2,1,1,1,1,1,1,2]
-GP_ADD = [[],[],[],[],[],[],[],[]]
+GP_ADD = [[0,1,2,3],[0,1,2,3],[0,1,2,3],[0,1,2,3],[0,1,2,3],[0,1,2,3],[0,1,2,3],[0,1,2,3]]
 X_EVAC_V = 4
 CB_V = []
 AHEAD = 3
@@ -51,7 +51,7 @@ def tile_yatnmn_kernel(tc, x, kernel, bias, alpha, out):
         grp = ctx.enter_context(tc.tile_pool(name="grp", bufs=2))
         codep = ctx.enter_context(tc.tile_pool(name="codep", bufs=3))
         smallp = ctx.enter_context(tc.tile_pool(name="smallp", bufs=3))
-        workp = ctx.enter_context(tc.tile_pool(name="workp", bufs=8))
+        workp = ctx.enter_context(tc.tile_pool(name="workp", bufs=10))
         psy = ctx.enter_context(tc.psum_pool(name="psy", bufs=4))
         pstr = ctx.enter_context(tc.psum_pool(name="pstr", bufs=2))
         psg = ctx.enter_context(tc.psum_pool(name="psg", bufs=1))

@@ -22,6 +22,7 @@ K_PASS = P * PACK
 PASSES = D // K_PASS
 CH = 512
 NCH = O // CH
+NT = NCH * MT
 BLK = 128
 NBLK = CH // BLK
 ROWS = PASSES * PACK
@@ -30,12 +31,14 @@ LN_C0 = 2.0404600064606253
 
 FLOPS = 2 * T * D * O
 
-GRAM = [2,1,1,1,1,1,1,2]
-GP_ADD = [[0,1,2,3],[0,1,2,3],[0,1,2,3],[0,1,2,3],[0,1,2,3],[0,1,2,3],[0,1,2,3],[0,1,2,3]]
-X_EVAC_V = 4
-CB_V = []
-AHEAD = 3
-MANUAL = False
+GRAM = [2,1,2,1,2,1,1,2]
+QS = 24
+QS_FROM = 6
+X_EVAC_S = []
+LR = 7
+LS = 6
+LMX = 2
+MANUAL = True
 
 
 def tile_yatnmn_kernel(tc, x, kernel, bias, alpha, out):
@@ -48,10 +51,10 @@ def tile_yatnmn_kernel(tc, x, kernel, bias, alpha, out):
             ctx.enter_context(tc.manual_schedule())
         const = ctx.enter_context(tc.tile_pool(name="const", bufs=1))
         rawp = ctx.enter_context(tc.tile_pool(name="rawp", bufs=4))
-        grp = ctx.enter_context(tc.tile_pool(name="grp", bufs=2))
+        grp = ctx.enter_context(tc.tile_pool(name="grp", bufs=4))
         codep = ctx.enter_context(tc.tile_pool(name="codep", bufs=3))
         smallp = ctx.enter_context(tc.tile_pool(name="smallp", bufs=3))
-        workp = ctx.enter_context(tc.tile_pool(name="workp", bufs=10))
+        workp = ctx.enter_context(tc.tile_pool(name="workp", bufs=6))
         psy = ctx.enter_context(tc.psum_pool(name="psy", bufs=4))
         pstr = ctx.enter_context(tc.psum_pool(name="pstr", bufs=2))
         psg = ctx.enter_context(tc.psum_pool(name="psg", bufs=1))
@@ -63,8 +66,17 @@ def tile_yatnmn_kernel(tc, x, kernel, bias, alpha, out):
         make_identity(nc, ident_f[:])
 
         raws = {}
+        gks = {}
         codes = {}
+        trs = {}
+        parts = {}
+        ksqs = {}
+        grams = {}
+        bcs = {}
         cbs = {}
+        ys = {}
+        ws = {}
+        xts = {}
 
         def load_pass(n, c):
             nc.sync.dma_start(
@@ -78,99 +90,159 @@ def tile_yatnmn_kernel(tc, x, kernel, bias, alpha, out):
             for c in range(PASSES):
                 load_pass(n, c)
 
-        def quant(n):
-            raw = raws[n]
-            gk = grp.tile([P, PASSES, PACK * CH], BF16, tag="gk", align_bytes=64)
-            kc = codep.tile([P, PASSES, CH], U32, align_bytes=64)
-            ksc = codep.tile([P, PASSES, CH], U8, align_bytes=64)
-            codes[n] = (kc, ksc)
+        def views(r):
+            n, c = divmod(r, PASSES)
+            dst = gks[r][:].rearrange("p (q i t) -> p q t i", i=4, t=PACK)
+            src = raws[n][:, c, :, :].rearrange("p t (q i) -> p q t i", i=4)
+            return dst, src
 
-            def regroup(c):
-                nc.vector.tensor_copy(
-                    out=gk[:, c, :].rearrange("p (q i t) -> p q t i", i=4, t=PACK),
-                    in_=raw[:, c, :, :].rearrange("p t (q i) -> p q t i", i=4))
+        def s_groups(r):
+            return QS if r >= QS_FROM else 0
 
-            def quantise(c):
-                nc.vector.quantize_mx(out=kc[:, c, :].bitcast(FP8X4), scales=ksc[:, c, :],
-                                      in_=gk[:, c, :])
+        def regroup_v(r):
+            gk = grp.tile([P, PACK * CH], BF16, tag="gk", align_bytes=64)
+            gks[r] = gk
+            dst, src = views(r)
+            qv = CH // 4 - s_groups(r)
+            nc.vector.tensor_copy(out=dst[:, 0:qv], in_=src[:, 0:qv])
 
-            regroup(0)
-            for c in range(1, PASSES):
-                regroup(c)
-                quantise(c - 1)
-            quantise(PASSES - 1)
+        def regroup_s(r):
+            dst, src = views(r)
+            qv = CH // 4 - s_groups(r)
+            if qv < CH // 4:
+                nc.scalar.copy(out=dst[:, qv:CH // 4], in_=src[:, qv:CH // 4])
 
-        def ksq_chunk(n):
-            raw = raws[n]
-            ng = GRAM[n]
-            ksq = smallp.tile([P, NBLK], F32)
-            part = smallp.tile([P, 2 * NBLK], F32)
+        def quantise(r):
+            n, c = divmod(r, PASSES)
+            if c == 0:
+                kc = codep.tile([P, PASSES, CH], U32, align_bytes=64)
+                ksc = codep.tile([P, PASSES, CH], U8, align_bytes=64)
+                codes[n] = (kc, ksc)
+            kc, ksc = codes[n]
+            nc.vector.quantize_mx(out=kc[:, c, :].bitcast(FP8X4), scales=ksc[:, c, :], in_=gks[r][:])
+
+        def banks(n):
+            return [(b, h) for h in range(2) for b in range(GRAM[n], NBLK)]
+
+        def bank_step(n, k):
+            return MT * n - LS + (k * MT) // len(banks(n))
+
+        def transposes(n, k):
+            b, h = banks(n)[k]
+            tr = pstr.tile([P, 8 * P], BF16)
+            trs[(n, k)] = tr
+            for i in range(8):
+                c, j = divmod(h * 8 + i, PACK)
+                nc.tensor.transpose(out=tr[:, i * P:(i + 1) * P],
+                                    in_=raws[n][:, c, j, b * BLK:(b + 1) * BLK],
+                                    identity=ident_b[:])
+
+        def squares(n, k):
+            b, h = banks(n)[k]
+            if k == 0:
+                part = smallp.tile([P, 2 * NBLK], F32)
+                parts[n] = part
+            idx = b * 2 + h
+            nc.scalar.activation(out=junk[:, 0:8 * P], in_=trs[(n, k)][:], func=ACT.Square,
+                                 accum_out=parts[n][:, idx:idx + 1])
+
+        def gram_blocks(n):
             gram = psg.tile([P, NBLK, P], F32)
-            for b in range(ng):
+            grams[n] = gram
+            for b in range(GRAM[n]):
                 for r in range(ROWS):
                     c, j = divmod(r, PACK)
-                    nc.tensor.matmul(out=gram[:, b, :], lhsT=raw[:, c, j, b * BLK:(b + 1) * BLK],
-                                     rhs=raw[:, c, j, b * BLK:(b + 1) * BLK],
+                    nc.tensor.matmul(out=gram[:, b, :], lhsT=raws[n][:, c, j, b * BLK:(b + 1) * BLK],
+                                     rhs=raws[n][:, c, j, b * BLK:(b + 1) * BLK],
                                      start=(r == 0), stop=(r == ROWS - 1))
-            for b in range(ng, NBLK):
-                for h in range(2):
-                    tr = pstr.tile([P, 8 * P], BF16)
-                    for i in range(8):
-                        c, j = divmod(h * 8 + i, PACK)
-                        nc.tensor.transpose(out=tr[:, i * P:(i + 1) * P],
-                                            in_=raw[:, c, j, b * BLK:(b + 1) * BLK],
-                                            identity=ident_b[:])
-                    idx = b * 2 + h
-                    nc.scalar.activation(out=junk[:, 0:8 * P], in_=tr[:], func=ACT.Square,
-                                         accum_out=part[:, idx:idx + 1])
+
+        def ksq_final(n):
+            ng = GRAM[n]
+            ksq = smallp.tile([P, NBLK], F32)
+            ksqs[n] = ksq
             for b in range(ng):
-                nc.vector.scalar_tensor_tensor(out=junkf[:], in0=gram[:, b, :], scalar=1.0, in1=ident_f[:],
-                                               op0=ALU.mult, op1=ALU.mult, accum_out=ksq[:, b:b + 1])
+                nc.vector.scalar_tensor_tensor(out=junkf[:], in0=grams[n][:, b, :], scalar=1.0,
+                                               in1=ident_f[:], op0=ALU.mult, op1=ALU.mult,
+                                               accum_out=ksq[:, b:b + 1])
             nc.vector.tensor_reduce(out=ksq[:, ng:NBLK],
-                                    in_=part[:, 2 * ng:2 * NBLK].rearrange("p (b h) -> p b h", h=2),
+                                    in_=parts[n][:, 2 * ng:2 * NBLK].rearrange("p (b h) -> p b h", h=2),
                                     axis=AX.X, op=ALU.add)
+
+        def spread(n):
             bc = psb.tile([P, CH], F32)
+            bcs[n] = bc
             for b in range(NBLK):
-                nc.tensor.matmul(out=bc[:, b * BLK:(b + 1) * BLK],
-                                 lhsT=ksq[:, b:b + 1].to_broadcast([P, P]), rhs=ident_f[:],
-                                 start=True, stop=True)
+                nc.tensor.transpose(out=bc[:, b * BLK:(b + 1) * BLK],
+                                    in_=ksqs[n][:, b:b + 1].to_broadcast([P, P]),
+                                    identity=ident_f[:])
+
+        def cb_copy(n):
             cb = smallp.tile([P, CH], F32)
             cbs[n] = cb
-            if n in CB_V:
-                nc.vector.tensor_scalar(out=cb[:], in0=bc[:], scalar1=0.5, scalar2=0.5 * EPS,
-                                        op0=ALU.mult, op1=ALU.add)
-            else:
-                nc.scalar.activation(out=cb[:], in_=bc[:], func=ACT.Copy, scale=0.5, bias=0.5 * EPS)
+            nc.scalar.activation(out=cb[:], in_=bcs[n][:], func=ACT.Copy, scale=0.5, bias=0.5 * EPS)
 
-        def mx_epilogue(n):
-            cols = slice(n * CH, (n + 1) * CH)
+        def mx(i):
+            n, mt = divmod(i, MT)
             kc, ksc = codes[n]
-            cb = cbs[n]
-            for mt in range(MT):
-                y = psy.tile([P, CH], F32, tag="y")
-                for c in range(PASSES):
-                    nc.tensor.matmul_mx(
-                        out=y[:],
-                        lhsT=xc[:, c, mt * P:(mt + 1) * P].bitcast(FP8X4),
-                        lhsT_scale=xsc[:, c, mt * P:(mt + 1) * P],
-                        rhs=kc[:, c, :].bitcast(FP8X4),
-                        rhs_scale=ksc[:, c, :],
-                        start=(c == 0), stop=(c == PASSES - 1))
-                w = workp.tile([P, CH], F32)
-                nc.vector.scalar_tensor_tensor(out=w[:], in0=y[:], scalar=xhalf[:, mt:mt + 1], in1=cb[:],
-                                               op0=ALU.subtract, op1=ALU.subtract)
-                nc.scalar.activation(out=w[:], in_=w[:], func=ACT.Abs_reciprocal_sqrt, scale=2.0)
-                nc.vector.tensor_tensor(out=w[:], in0=y[:], in1=w[:], op=ALU.mult)
-                nc.scalar.activation(out=w[:], in_=w[:], func=ACT.Square, scale=sqs[:, 0:1])
-                if mt in GP_ADD[n]:
-                    nc.gpsimd.tensor_tensor(out=w[:], in0=w[:], in1=bs[:, cols], op=ALU.add)
+            y = psy.tile([P, CH], F32, tag="y")
+            ys[i] = y
+            for c in range(PASSES):
+                nc.tensor.matmul_mx(
+                    out=y[:],
+                    lhsT=xc[:, c, mt * P:(mt + 1) * P].bitcast(FP8X4),
+                    lhsT_scale=xsc[:, c, mt * P:(mt + 1) * P],
+                    rhs=kc[:, c, :].bitcast(FP8X4),
+                    rhs_scale=ksc[:, c, :],
+                    start=(c == 0), stop=(c == PASSES - 1))
+
+        def v1(i):
+            n, mt = divmod(i, MT)
+            w = workp.tile([P, CH], F32)
+            ws[i] = w
+            nc.vector.scalar_tensor_tensor(out=w[:], in0=ys[i][:], scalar=xhalf[:, mt:mt + 1],
+                                           in1=cbs[n][:], op0=ALU.subtract, op1=ALU.subtract)
+
+        def s1(i):
+            nc.scalar.activation(out=ws[i][:], in_=ws[i][:], func=ACT.Abs_reciprocal_sqrt, scale=2.0)
+
+        def v2(i):
+            nc.vector.tensor_tensor(out=ws[i][:], in0=ys[i][:], in1=ws[i][:], op=ALU.mult)
+
+        def s2(i):
+            nc.scalar.activation(out=ws[i][:], in_=ws[i][:], func=ACT.Square, scale=sqs[:, 0:1])
+
+        def v3(i):
+            n, mt = divmod(i, MT)
+            cols = slice(n * CH, (n + 1) * CH)
+            nc.vector.scalar_tensor_tensor(out=ws[i][:], in0=bias_b[:, cols], scalar=sfac[:, 0:1],
+                                           in1=ws[i][:], op0=ALU.mult, op1=ALU.add)
+            if n == NCH - 1:
+                nc.sync.dma_start(out=of[mt * P:(mt + 1) * P, cols], in_=ws[i][:])
+            else:
+                nc.gpsimd.dma_start(out=of[mt * P:(mt + 1) * P, cols], in_=ws[i][:])
+
+        def x_transposes(half):
+            for c in range(PASSES):
+                xt = psy.tile([P, 2, 2 * P], F32, tag="y")
+                xts[(c, half)] = xt
+                for u in range(2):
+                    for ml in range(2):
+                        nc.tensor.transpose(out=xt[:, u, ml * P:(ml + 1) * P],
+                                            in_=xw[:, 2 * half + ml, c, :, u],
+                                            identity=ident_f[:])
+
+        def x_copies(half):
+            for c in range(PASSES):
+                dst = gx32[:, c, half * 2 * P:(half + 1) * 2 * P, :]
+                src = xts[(c, half)][:].rearrange("p u t -> p t u")
+                if c in X_EVAC_S:
+                    nc.scalar.copy(out=dst, in_=src)
                 else:
-                    nc.vector.scalar_tensor_tensor(out=w[:], in0=bias_b[:, cols], scalar=sfac[:, 0:1],
-                                                   in1=w[:], op0=ALU.mult, op1=ALU.add)
-                if n == NCH - 1:
-                    nc.sync.dma_start(out=of[mt * P:(mt + 1) * P, cols], in_=w[:])
-                else:
-                    nc.gpsimd.dma_start(out=of[mt * P:(mt + 1) * P, cols], in_=w[:])
+                    nc.vector.tensor_copy(out=dst, in_=src)
+
+        def x_square(mt):
+            nc.scalar.activation(out=junk[:], in_=x_sb[:, mt, :], func=ACT.Square,
+                                 accum_out=xs_raw[:, mt:mt + 1])
 
         al = const.tile([P, 1], BF16)
         nc.scalar.dma_start(out=al[:], in_=alpha.partition_broadcast(P))
@@ -180,10 +252,10 @@ def tile_yatnmn_kernel(tc, x, kernel, bias, alpha, out):
         for i in range(MT):
             load_pass(0, i)
             nc.sync.dma_start(out=x_sb[:, i, :], in_=xf[i * P:(i + 1) * P, :])
+        load(1)
         bias_b = const.tile([P, O], BF16)
         nc.sync.dma_start(out=bias_b[:], in_=bias.partition_broadcast(P))
-        for n in range(1, AHEAD):
-            load(n)
+        load(2)
 
         sqs = const.tile([P, 1], F32)
         nc.scalar.activation(out=sqs[:], in_=al[:], func=ACT.Exp, scale=0.5 * LN_C0)
@@ -191,48 +263,66 @@ def tile_yatnmn_kernel(tc, x, kernel, bias, alpha, out):
         nc.scalar.activation(out=sfac[:], in_=al[:], func=ACT.Exp, scale=LN_C0)
         junk = const.tile([P, D], BF16)
         junkf = const.tile([P, P], F32)
-        if any(len(g) > 0 for g in GP_ADD):
-            bs = const.tile([P, O], F32)
-            nc.gpsimd.tensor_scalar(out=bs[:], in0=bias_b[:], scalar1=sfac[:, 0:1], scalar2=0.0,
-                                    op0=ALU.mult, op1=ALU.add)
-
-        quant(0)
-
+        xs_raw = const.tile([P, MT], F32)
+        xhalf = const.tile([P, MT], F32)
         xw = x_sb[:].bitcast(F32).rearrange("p m (c q u) -> p m c q u", c=PASSES, q=P, u=2)
-        gx = grp.tile([P, PASSES, PACK * T], BF16, tag="gk", align_bytes=64)
+        gx = const.tile([P, PASSES, PACK * T], BF16, align_bytes=64)
         gx32 = gx[:].bitcast(F32).rearrange("p c (t u) -> p c t u", u=2)
         xc = const.tile([P, PASSES, T], U32, align_bytes=64)
         xsc = const.tile([P, PASSES, T], U8, align_bytes=64)
-        for c in range(PASSES):
-            for half in range(2):
-                xt = psy.tile([P, 2, 2 * P], F32, tag="y")
-                for u in range(2):
-                    for ml in range(2):
-                        nc.tensor.transpose(out=xt[:, u, ml * P:(ml + 1) * P],
-                                            in_=xw[:, 2 * half + ml, c, :, u],
-                                            identity=ident_f[:])
-                dst = gx32[:, c, half * 2 * P:(half + 1) * 2 * P, :]
-                src = xt[:].rearrange("p u t -> p t u")
-                if c * 2 + half < X_EVAC_V:
-                    nc.vector.tensor_copy(out=dst, in_=src)
-                else:
-                    nc.scalar.copy(out=dst, in_=src)
-        for c in range(PASSES):
-            nc.vector.quantize_mx(out=xc[:, c, :].bitcast(FP8X4), scales=xsc[:, c, :], in_=gx[:, c, :])
 
-        ksq_chunk(0)
-
-        xs_raw = const.tile([P, MT], F32)
-        for mt in range(MT):
-            nc.scalar.activation(out=junk[:], in_=x_sb[:, mt, :], func=ACT.Square,
-                                 accum_out=xs_raw[:, mt:mt + 1])
-        xhalf = const.tile([P, MT], F32)
-        nc.vector.tensor_scalar(out=xhalf[:], in0=xs_raw[:], scalar1=0.5, scalar2=None, op0=ALU.mult)
-
-        for n in range(NCH):
-            if n + AHEAD < NCH:
-                load(n + AHEAD)
-            if n + 1 < NCH:
-                quant(n + 1)
-                ksq_chunk(n + 1)
-            mx_epilogue(n)
+        first = -max(LR, LS + 1)
+        for i in range(first, NT + 2):
+            if (i + 15) % MT == 0 and 3 <= (i + 15) // MT < NCH:
+                load((i + 15) // MT)
+            if 0 <= i + LMX < NT:
+                mx(i + LMX)
+            if 0 <= i < NT:
+                v1(i)
+            if 0 <= i - 1 < NT:
+                v2(i - 1)
+            if 0 <= i - 2 < NT:
+                v3(i - 2)
+            if 0 <= i < NT:
+                s1(i)
+            if 0 <= i - 1 < NT:
+                s2(i - 1)
+            fin = (i + 2) // MT
+            if (i + 2) % MT == 0 and 0 <= fin < NCH:
+                ksq_final(fin)
+            if i == -1:
+                nc.vector.tensor_scalar(out=xhalf[:], in0=xs_raw[:], scalar1=0.5, scalar2=None,
+                                        op0=ALU.mult)
+            r = i + LR
+            if 0 <= r < NCH * PASSES:
+                regroup_v(r)
+            if 0 <= r - 1 < NCH * PASSES:
+                quantise(r - 1)
+            if i == -6:
+                x_transposes(0)
+                x_copies(0)
+            if i == -4:
+                x_transposes(1)
+                x_copies(1)
+            if i == -3:
+                for c in range(PASSES):
+                    nc.vector.quantize_mx(out=xc[:, c, :].bitcast(FP8X4), scales=xsc[:, c, :],
+                                          in_=gx[:, c, :])
+            if (i + 1) % MT == 0 and (i + 1) // MT < NCH and i + 1 >= 0:
+                cb_copy((i + 1) // MT)
+            if 0 <= r < NCH * PASSES:
+                regroup_s(r)
+            for n in range(NCH):
+                for k in range(len(banks(n))):
+                    if bank_step(n, k) == i:
+                        squares(n, k)
+            if -7 <= i <= -4:
+                x_square(i + 7)
+            if (i + 2) % MT == 0 and 0 <= fin < NCH:
+                spread(fin)
+            for n in range(NCH):
+                for k in range(len(banks(n))):
+                    if bank_step(n, k) == i + 1:
+                        transposes(n, k)
+            if (i + 4) % MT == 0 and 0 <= (i + 4) // MT < NCH:
+                gram_blocks((i + 4) // MT)

@@ -32,8 +32,10 @@ LN_C0 = 2.0404600064606253
 FLOPS = 2 * T * D * O
 
 GRAM = [2,1,2,1,2,1,1,2]
-QS = 24
+QS = 20
 QS_FROM = 6
+QG = 44
+QG_FROM = 7
 X_EVAC_S = []
 LR = 7
 LS = 6
@@ -51,7 +53,7 @@ def tile_yatnmn_kernel(tc, x, kernel, bias, alpha, out):
             ctx.enter_context(tc.manual_schedule())
         const = ctx.enter_context(tc.tile_pool(name="const", bufs=1))
         rawp = ctx.enter_context(tc.tile_pool(name="rawp", bufs=4))
-        grp = ctx.enter_context(tc.tile_pool(name="grp", bufs=4))
+        grp = ctx.enter_context(tc.tile_pool(name="grp", bufs=2))
         codep = ctx.enter_context(tc.tile_pool(name="codep", bufs=3))
         smallp = ctx.enter_context(tc.tile_pool(name="smallp", bufs=3))
         workp = ctx.enter_context(tc.tile_pool(name="workp", bufs=6))
@@ -99,18 +101,31 @@ def tile_yatnmn_kernel(tc, x, kernel, bias, alpha, out):
         def s_groups(r):
             return QS if r >= QS_FROM else 0
 
-        def regroup_v(r):
+        def g_groups(r):
+            return QG if r >= QG_FROM else 0
+
+        def regroup_g(r):
             gk = grp.tile([P, PACK * CH], BF16, tag="gk", align_bytes=64)
             gks[r] = gk
+            n, c = divmod(r, PASSES)
+            c0 = CH - 4 * g_groups(r)
+            if c0 < CH:
+                nc.gpsimd.tensor_scalar(
+                    out=gk[:, PACK * c0:PACK * CH].rearrange("p (w t) -> p w t", t=PACK),
+                    in0=raws[n][:, c, :, c0:CH].rearrange("p t w -> p w t"),
+                    scalar1=1.0, scalar2=0.0, op0=ALU.mult, op1=ALU.add)
+
+        def regroup_v(r):
             dst, src = views(r)
-            qv = CH // 4 - s_groups(r)
+            qv = CH // 4 - s_groups(r) - g_groups(r)
             nc.vector.tensor_copy(out=dst[:, 0:qv], in_=src[:, 0:qv])
 
         def regroup_s(r):
             dst, src = views(r)
-            qv = CH // 4 - s_groups(r)
-            if qv < CH // 4:
-                nc.scalar.copy(out=dst[:, qv:CH // 4], in_=src[:, qv:CH // 4])
+            qv = CH // 4 - s_groups(r) - g_groups(r)
+            qe = CH // 4 - g_groups(r)
+            if qv < qe:
+                nc.scalar.copy(out=dst[:, qv:qe], in_=src[:, qv:qe])
 
         def quantise(r):
             n, c = divmod(r, PASSES)
@@ -216,10 +231,7 @@ def tile_yatnmn_kernel(tc, x, kernel, bias, alpha, out):
             cols = slice(n * CH, (n + 1) * CH)
             nc.vector.scalar_tensor_tensor(out=ws[i][:], in0=bias_b[:, cols], scalar=sfac[:, 0:1],
                                            in1=ws[i][:], op0=ALU.mult, op1=ALU.add)
-            if n == NCH - 1:
-                nc.sync.dma_start(out=of[mt * P:(mt + 1) * P, cols], in_=ws[i][:])
-            else:
-                nc.gpsimd.dma_start(out=of[mt * P:(mt + 1) * P, cols], in_=ws[i][:])
+            nc.sync.dma_start(out=of[mt * P:(mt + 1) * P, cols], in_=ws[i][:])
 
         def x_transposes(half):
             for c in range(PASSES):
@@ -277,12 +289,13 @@ def tile_yatnmn_kernel(tc, x, kernel, bias, alpha, out):
                 load((i + 15) // MT)
             if 0 <= i + LMX < NT:
                 mx(i + LMX)
+            r = i + LR
+            if 0 <= r < NCH * PASSES:
+                regroup_g(r)
             if 0 <= i < NT:
                 v1(i)
             if 0 <= i - 1 < NT:
                 v2(i - 1)
-            if 0 <= i - 2 < NT:
-                v3(i - 2)
             if 0 <= i < NT:
                 s1(i)
             if 0 <= i - 1 < NT:
@@ -293,7 +306,8 @@ def tile_yatnmn_kernel(tc, x, kernel, bias, alpha, out):
             if i == -1:
                 nc.vector.tensor_scalar(out=xhalf[:], in0=xs_raw[:], scalar1=0.5, scalar2=None,
                                         op0=ALU.mult)
-            r = i + LR
+            if 0 <= i - 2 < NT:
+                v3(i - 2)
             if 0 <= r < NCH * PASSES:
                 regroup_v(r)
             if 0 <= r - 1 < NCH * PASSES:

@@ -37,6 +37,7 @@ QS_FROM = 6
 QG = 44
 QG_FROM = 7
 X_EVAC_S = []
+G3_FROM = 24
 LR = 7
 LS = 6
 LMX = 2
@@ -229,8 +230,12 @@ def tile_yatnmn_kernel(tc, x, kernel, bias, alpha, out):
         def v3(i):
             n, mt = divmod(i, MT)
             cols = slice(n * CH, (n + 1) * CH)
-            nc.vector.scalar_tensor_tensor(out=ws[i][:], in0=bias_b[:, cols], scalar=sfac[:, 0:1],
-                                           in1=ws[i][:], op0=ALU.mult, op1=ALU.add)
+            if i >= G3_FROM:
+                lo = n * CH - (G3_FROM // MT) * CH
+                nc.gpsimd.tensor_tensor(out=ws[i][:], in0=ws[i][:], in1=bprime[:, lo:lo + CH], op=ALU.add)
+            else:
+                nc.vector.scalar_tensor_tensor(out=ws[i][:], in0=bias_b[:, cols], scalar=sfac[:, 0:1],
+                                               in1=ws[i][:], op0=ALU.mult, op1=ALU.add)
             nc.sync.dma_start(out=of[mt * P:(mt + 1) * P, cols], in_=ws[i][:])
 
         def x_transposes(half):
@@ -273,6 +278,7 @@ def tile_yatnmn_kernel(tc, x, kernel, bias, alpha, out):
         nc.scalar.activation(out=sqs[:], in_=al[:], func=ACT.Exp, scale=0.5 * LN_C0)
         sfac = const.tile([P, 1], F32)
         nc.scalar.activation(out=sfac[:], in_=al[:], func=ACT.Exp, scale=LN_C0)
+        bprime = const.tile([P, O - (G3_FROM // MT) * CH], F32)
         junk = const.tile([P, D], BF16)
         junkf = const.tile([P, P], F32)
         xs_raw = const.tile([P, MT], F32)
@@ -326,6 +332,9 @@ def tile_yatnmn_kernel(tc, x, kernel, bias, alpha, out):
                 cb_copy((i + 1) // MT)
             if 0 <= r < NCH * PASSES:
                 regroup_s(r)
+            if i == G3_FROM:
+                nc.scalar.activation(out=bprime[:], in_=bias_b[:, (G3_FROM // MT) * CH:O], func=ACT.Copy,
+                                     scale=sfac[:, 0:1])
             for n in range(NCH):
                 for k in range(len(banks(n))):
                     if bank_step(n, k) == i:

@@ -32,9 +32,11 @@ LN_C0 = 2.0404600064606253
 FLOPS = 2 * T * D * O
 
 GRAM = [2,1,2,1,2,1,1,2]
-QS = 20
+QS = 8
 QS_FROM = 6
 QG = 44
+QG_X = 96
+X_STEPS = (-6, -4)
 QG_FROM = 7
 X_EVAC_S = []
 G3_FROM = 24
@@ -103,6 +105,8 @@ def tile_yatnmn_kernel(tc, x, kernel, bias, alpha, out):
             return QS if r >= QS_FROM else 0
 
         def g_groups(r):
+            if r - LR - 1 in X_STEPS:
+                return QG_X
             return QG if r >= QG_FROM else 0
 
         def regroup_g(r):
@@ -230,7 +234,7 @@ def tile_yatnmn_kernel(tc, x, kernel, bias, alpha, out):
         def v3(i):
             n, mt = divmod(i, MT)
             cols = slice(n * CH, (n + 1) * CH)
-            if i >= G3_FROM:
+            if i >= G3_FROM and mt < MT - 1:
                 lo = n * CH - (G3_FROM // MT) * CH
                 nc.gpsimd.tensor_tensor(out=ws[i][:], in0=ws[i][:], in1=bprime[:, lo:lo + CH], op=ALU.add)
             else:
@@ -318,12 +322,9 @@ def tile_yatnmn_kernel(tc, x, kernel, bias, alpha, out):
                 regroup_v(r)
             if 0 <= r - 1 < NCH * PASSES:
                 quantise(r - 1)
-            if i == -6:
-                x_transposes(0)
-                x_copies(0)
-            if i == -4:
-                x_transposes(1)
-                x_copies(1)
+            if i in X_STEPS:
+                x_transposes(X_STEPS.index(i))
+                x_copies(X_STEPS.index(i))
             if i == -3:
                 for c in range(PASSES):
                     nc.vector.quantize_mx(out=xc[:, c, :].bitcast(FP8X4), scales=xsc[:, c, :],

@@ -34,7 +34,7 @@ FLOPS = 2 * T * D * O
 GRAM = [2,1,2,1,2,1,1,2]
 QS = 8
 QS_FROM = 6
-QG = 44
+QG = 52
 QG_X = 96
 X_STEPS = (-6, -4)
 QG_FROM = 7
@@ -283,6 +283,8 @@ def tile_yatnmn_kernel(tc, x, kernel, bias, alpha, out):
         sfac = const.tile([P, 1], F32)
         nc.scalar.activation(out=sfac[:], in_=al[:], func=ACT.Exp, scale=LN_C0)
         bprime = const.tile([P, O - (G3_FROM // MT) * CH], F32)
+        warm = const.tile([P, 1], F32)
+        nc.scalar.activation(out=warm[:], in_=sfac[:], func=ACT.Abs_reciprocal_sqrt)
         junk = const.tile([P, D], BF16)
         junkf = const.tile([P, P], F32)
         xs_raw = const.tile([P, MT], F32)
@@ -318,10 +320,10 @@ def tile_yatnmn_kernel(tc, x, kernel, bias, alpha, out):
                                         op0=ALU.mult)
             if 0 <= i - 2 < NT:
                 v3(i - 2)
-            if 0 <= r < NCH * PASSES:
-                regroup_v(r)
             if 0 <= r - 1 < NCH * PASSES:
                 quantise(r - 1)
+            if 0 <= r < NCH * PASSES:
+                regroup_v(r)
             if i in X_STEPS:
                 x_transposes(X_STEPS.index(i))
                 x_copies(X_STEPS.index(i))

@@ -308,13 +308,13 @@ def tile_yatnmn_kernel(tc, x, kernel, bias, alpha, out):
                 v1(i)
             if 0 <= i - 1 < NT:
                 v2(i - 1)
+            if (i + 1) % MT == 0 and (i + 1) // MT < NCH and i + 1 >= 0:
+                cb_copy((i + 1) // MT)
             if 0 <= i < NT:
                 s1(i)
             if 0 <= i - 1 < NT:
                 s2(i - 1)
             fin = (i + 2) // MT
-            if (i + 2) % MT == 0 and 0 <= fin < NCH:
-                ksq_final(fin)
             if i == -1:
                 nc.vector.tensor_scalar(out=xhalf[:], in0=xs_raw[:], scalar1=0.5, scalar2=None,
                                         op0=ALU.mult)
@@ -324,6 +324,8 @@ def tile_yatnmn_kernel(tc, x, kernel, bias, alpha, out):
                 quantise(r - 1)
             if 0 <= r < NCH * PASSES:
                 regroup_v(r)
+            if (i + 2) % MT == 0 and 0 <= fin < NCH:
+                ksq_final(fin)
             if i in X_STEPS:
                 x_transposes(X_STEPS.index(i))
                 x_copies(X_STEPS.index(i))
@@ -331,8 +333,6 @@ def tile_yatnmn_kernel(tc, x, kernel, bias, alpha, out):
                 for c in range(PASSES):
                     nc.vector.quantize_mx(out=xc[:, c, :].bitcast(FP8X4), scales=xsc[:, c, :],
                                           in_=gx[:, c, :])
-            if (i + 1) % MT == 0 and (i + 1) // MT < NCH and i + 1 >= 0:
-                cb_copy((i + 1) // MT)
             if 0 <= r < NCH * PASSES:
                 regroup_s(r)
             if i == G3_FROM:

@@ -37,6 +37,7 @@ QS_FROM = 6
 QG = 52
 QG_X = 96
 X_STEPS = (-6, -4)
+XC_STEPS = (-5, -3)
 QG_FROM = 7
 X_EVAC_S = []
 G3_FROM = 24
@@ -105,7 +106,7 @@ def tile_yatnmn_kernel(tc, x, kernel, bias, alpha, out):
             return QS if r >= QS_FROM else 0
 
         def g_groups(r):
-            if r - LR - 1 in X_STEPS:
+            if r - LR - 1 in XC_STEPS:
                 return QG_X
             return QG if r >= QG_FROM else 0
 
@@ -145,7 +146,18 @@ def tile_yatnmn_kernel(tc, x, kernel, bias, alpha, out):
             return [(b, h) for h in range(2) for b in range(GRAM[n], NBLK)]
 
         def bank_step(n, k):
+            if n == 0:
+                return -LS + k // 2
             return MT * n - LS + (k * MT) // len(banks(n))
+
+        def sum_step(n):
+            return MT * n - 2 if n else -3
+
+        def copy_step(n):
+            return MT * n - 1 if n else -2
+
+        def gram_step(n):
+            return MT * n - 4 if n else -5
 
         def transposes(n, k):
             b, h = banks(n)[k]
@@ -304,17 +316,20 @@ def tile_yatnmn_kernel(tc, x, kernel, bias, alpha, out):
             r = i + LR
             if 0 <= r < NCH * PASSES:
                 regroup_g(r)
+            if i == G3_FROM + 1:
+                nc.gpsimd.tensor_scalar(out=bprime[:], in0=bias_b[:, (G3_FROM // MT) * CH:O], scalar1=sfac[:, 0:1],
+                                        scalar2=0.0, op0=ALU.mult, op1=ALU.add)
             if 0 <= i < NT:
                 v1(i)
             if 0 <= i - 1 < NT:
                 v2(i - 1)
-            if (i + 1) % MT == 0 and (i + 1) // MT < NCH and i + 1 >= 0:
-                cb_copy((i + 1) // MT)
+            for n in range(NCH):
+                if copy_step(n) == i:
+                    cb_copy(n)
             if 0 <= i < NT:
                 s1(i)
             if 0 <= i - 1 < NT:
                 s2(i - 1)
-            fin = (i + 2) // MT
             if i == -1:
                 nc.vector.tensor_scalar(out=xhalf[:], in0=xs_raw[:], scalar1=0.5, scalar2=None,
                                         op0=ALU.mult)
@@ -324,31 +339,32 @@ def tile_yatnmn_kernel(tc, x, kernel, bias, alpha, out):
                 quantise(r - 1)
             if 0 <= r < NCH * PASSES:
                 regroup_v(r)
-            if (i + 2) % MT == 0 and 0 <= fin < NCH:
-                ksq_final(fin)
+            for n in range(NCH):
+                if sum_step(n) == i:
+                    ksq_final(n)
             if i in X_STEPS:
                 x_transposes(X_STEPS.index(i))
-                x_copies(X_STEPS.index(i))
+            if i in XC_STEPS:
+                x_copies(XC_STEPS.index(i))
             if i == -3:
                 for c in range(PASSES):
                     nc.vector.quantize_mx(out=xc[:, c, :].bitcast(FP8X4), scales=xsc[:, c, :],
                                           in_=gx[:, c, :])
             if 0 <= r < NCH * PASSES:
                 regroup_s(r)
-            if i == G3_FROM:
-                nc.scalar.activation(out=bprime[:], in_=bias_b[:, (G3_FROM // MT) * CH:O], func=ACT.Copy,
-                                     scale=sfac[:, 0:1])
             for n in range(NCH):
                 for k in range(len(banks(n))):
                     if bank_step(n, k) == i:
                         squares(n, k)
             if -7 <= i <= -4:
                 x_square(i + 7)
-            if (i + 2) % MT == 0 and 0 <= fin < NCH:
-                spread(fin)
+            for n in range(NCH):
+                if sum_step(n) == i:
+                    spread(n)
             for n in range(NCH):
                 for k in range(len(banks(n))):
                     if bank_step(n, k) == i + 1:
                         transposes(n, k)
-            if (i + 4) % MT == 0 and 0 <= (i + 4) // MT < NCH:
-                gram_blocks((i + 4) // MT)
+            for n in range(NCH):
+                if gram_step(n) == i:
+                    gram_blocks(n)

@@ -34,7 +34,7 @@ FLOPS = 2 * T * D * O
 GRAM = [2,1,2,1,2,1,1,2]
 QS = 8
 QS_FROM = 6
-QG = 52
+QG = 72
 QG_X = 96
 X_STEPS = (-6, -4)
 XC_STEPS = (-5, -3)
@@ -63,8 +63,8 @@ def tile_yatnmn_kernel(tc, x, kernel, bias, alpha, out):
         workp = ctx.enter_context(tc.tile_pool(name="workp", bufs=6))
         psy = ctx.enter_context(tc.psum_pool(name="psy", bufs=4))
         pstr = ctx.enter_context(tc.psum_pool(name="pstr", bufs=2))
-        psg = ctx.enter_context(tc.psum_pool(name="psg", bufs=1))
-        psb = ctx.enter_context(tc.psum_pool(name="psb", bufs=1))
+        psk = ctx.enter_context(tc.psum_pool(name="psk", bufs=1))
+        psbias = ctx.enter_context(tc.psum_pool(name="psbias", bufs=1))
 
         ident_b = const.tile([P, P], BF16)
         make_identity(nc, ident_b[:])
@@ -179,7 +179,7 @@ def tile_yatnmn_kernel(tc, x, kernel, bias, alpha, out):
                                  accum_out=parts[n][:, idx:idx + 1])
 
         def gram_blocks(n):
-            gram = psg.tile([P, NBLK, P], F32)
+            gram = psk.tile([P, NBLK, P], F32, tag="k")
             grams[n] = gram
             for b in range(GRAM[n]):
                 for r in range(ROWS):
@@ -201,7 +201,7 @@ def tile_yatnmn_kernel(tc, x, kernel, bias, alpha, out):
                                     axis=AX.X, op=ALU.add)
 
         def spread(n):
-            bc = psb.tile([P, CH], F32)
+            bc = psk.tile([P, CH], F32, tag="k")
             bcs[n] = bc
             for b in range(NBLK):
                 nc.tensor.transpose(out=bc[:, b * BLK:(b + 1) * BLK],
@@ -212,6 +212,12 @@ def tile_yatnmn_kernel(tc, x, kernel, bias, alpha, out):
             cb = smallp.tile([P, CH], F32)
             cbs[n] = cb
             nc.scalar.activation(out=cb[:], in_=bcs[n][:], func=ACT.Copy, scale=0.5, bias=0.5 * EPS)
+
+        def bias_spread(n):
+            for b in range(NBLK):
+                nc.tensor.transpose(out=bias_ps[:, n % 2, b * BLK:(b + 1) * BLK],
+                                    in_=bias_t[:, NBLK * n + b:NBLK * n + b + 1].to_broadcast([P, P]),
+                                    identity=ident_b[:])
 
         def mx(i):
             n, mt = divmod(i, MT)
@@ -250,7 +256,7 @@ def tile_yatnmn_kernel(tc, x, kernel, bias, alpha, out):
                 lo = n * CH - (G3_FROM // MT) * CH
                 nc.gpsimd.tensor_tensor(out=ws[i][:], in0=ws[i][:], in1=bprime[:, lo:lo + CH], op=ALU.add)
             else:
-                nc.vector.scalar_tensor_tensor(out=ws[i][:], in0=bias_b[:, cols], scalar=sfac[:, 0:1],
+                nc.vector.scalar_tensor_tensor(out=ws[i][:], in0=bias_ps[:, n % 2, :], scalar=sfac[:, 0:1],
                                                in1=ws[i][:], op0=ALU.mult, op1=ALU.add)
             nc.sync.dma_start(out=of[mt * P:(mt + 1) * P, cols], in_=ws[i][:])
 
@@ -282,13 +288,19 @@ def tile_yatnmn_kernel(tc, x, kernel, bias, alpha, out):
         raw0 = rawp.tile([P, PASSES, PACK, CH], BF16, tag="raw")
         raws[0] = raw0
         x_sb = rawp.tile([P, MT, D], BF16, tag="raw")
+        bias_rows = const.tile([P, P], BF16)
+        nc.gpsimd.memset(bias_rows[:], 0.0)
         for i in range(MT):
             load_pass(0, i)
             nc.sync.dma_start(out=x_sb[:, i, :], in_=xf[i * P:(i + 1) * P, :])
+            if i == 0:
+                nc.sync.dma_start(out=bias_rows[0:O // P, :], in_=bias.rearrange("(j q) -> j q", q=P))
         load(1)
-        bias_b = const.tile([P, O], BF16)
-        nc.sync.dma_start(out=bias_b[:], in_=bias.partition_broadcast(P))
         load(2)
+        bias_b = const.tile([P, O - (G3_FROM // MT) * CH], BF16)
+        nc.sync.dma_start(out=bias_b[:], in_=bias[(G3_FROM // MT) * CH:O].partition_broadcast(P))
+        bias_ps = psbias.tile([P, 2, CH], BF16)
+        bias_t = const.tile([P, O // P], BF16)
 
         sqs = const.tile([P, 1], F32)
         nc.scalar.activation(out=sqs[:], in_=al[:], func=ACT.Exp, scale=0.5 * LN_C0)
@@ -317,7 +329,7 @@ def tile_yatnmn_kernel(tc, x, kernel, bias, alpha, out):
             if 0 <= r < NCH * PASSES:
                 regroup_g(r)
             if i == G3_FROM + 1:
-                nc.gpsimd.tensor_scalar(out=bprime[:], in0=bias_b[:, (G3_FROM // MT) * CH:O], scalar1=sfac[:, 0:1],
+                nc.gpsimd.tensor_scalar(out=bprime[:], in0=bias_b[:], scalar1=sfac[:, 0:1],
                                         scalar2=0.0, op0=ALU.mult, op1=ALU.add)
             if 0 <= i < NT:
                 v1(i)
@@ -342,6 +354,8 @@ def tile_yatnmn_kernel(tc, x, kernel, bias, alpha, out):
             for n in range(NCH):
                 if sum_step(n) == i:
                     ksq_final(n)
+            if i == -4:
+                nc.vector.tensor_copy(out=bias_t[:], in_=bias_ps[:, 1, 0:O // P])
             if i in X_STEPS:
                 x_transposes(X_STEPS.index(i))
             if i in XC_STEPS:
@@ -358,9 +372,12 @@ def tile_yatnmn_kernel(tc, x, kernel, bias, alpha, out):
                         squares(n, k)
             if -7 <= i <= -4:
                 x_square(i + 7)
+            if i == -6:
+                nc.tensor.transpose(out=bias_ps[:, 1, 0:P], in_=bias_rows[:], identity=ident_b[:])
             for n in range(NCH):
                 if sum_step(n) == i:
                     spread(n)
+                    bias_spread(n)
             for n in range(NCH):
                 for k in range(len(banks(n))):
                     if bank_step(n, k) == i + 1:

@@ -175,7 +175,7 @@ def tile_yatnmn_kernel(tc, x, kernel, bias, alpha, out):
                 part = smallp.tile([P, 2 * NBLK], F32)
                 parts[n] = part
             idx = b * 2 + h
-            nc.scalar.activation(out=junk[:, 0:8 * P], in_=trs[(n, k)][:], func=ACT.Square,
+            nc.scalar.activation(out=junk[:, k % 2, 0:8 * P], in_=trs[(n, k)][:], func=ACT.Square,
                                  accum_out=parts[n][:, idx:idx + 1])
 
         def gram_blocks(n):
@@ -193,7 +193,7 @@ def tile_yatnmn_kernel(tc, x, kernel, bias, alpha, out):
             ksq = smallp.tile([P, NBLK], F32)
             ksqs[n] = ksq
             for b in range(ng):
-                nc.vector.scalar_tensor_tensor(out=junkf[:], in0=grams[n][:, b, :], scalar=1.0,
+                nc.vector.scalar_tensor_tensor(out=junkf[:, b, :], in0=grams[n][:, b, :], scalar=1.0,
                                                in1=ident_f[:], op0=ALU.mult, op1=ALU.mult,
                                                accum_out=ksq[:, b:b + 1])
             nc.vector.tensor_reduce(out=ksq[:, ng:NBLK],
@@ -233,32 +233,44 @@ def tile_yatnmn_kernel(tc, x, kernel, bias, alpha, out):
                     rhs_scale=ksc[:, c, :],
                     start=(c == 0), stop=(c == PASSES - 1))
 
+        def pieces(i):
+            if i == NT - 1:
+                return [slice(0, CH // 2), slice(CH // 2, CH)]
+            return [slice(0, CH)]
+
         def v1(i):
             n, mt = divmod(i, MT)
             w = workp.tile([P, CH], F32)
             ws[i] = w
-            nc.vector.scalar_tensor_tensor(out=w[:], in0=ys[i][:], scalar=xhalf[:, mt:mt + 1],
-                                           in1=cbs[n][:], op0=ALU.subtract, op1=ALU.subtract)
+            for s in pieces(i):
+                nc.vector.scalar_tensor_tensor(out=w[:, s], in0=ys[i][:, s], scalar=xhalf[:, mt:mt + 1],
+                                               in1=cbs[n][:, s], op0=ALU.subtract, op1=ALU.subtract)
 
         def s1(i):
-            nc.scalar.activation(out=ws[i][:], in_=ws[i][:], func=ACT.Abs_reciprocal_sqrt, scale=2.0)
+            for s in pieces(i):
+                nc.scalar.activation(out=ws[i][:, s], in_=ws[i][:, s], func=ACT.Abs_reciprocal_sqrt, scale=2.0)
 
         def v2(i):
-            nc.vector.tensor_tensor(out=ws[i][:], in0=ys[i][:], in1=ws[i][:], op=ALU.mult)
+            for s in pieces(i):
+                nc.vector.tensor_tensor(out=ws[i][:, s], in0=ys[i][:, s], in1=ws[i][:, s], op=ALU.mult)
 
         def s2(i):
-            nc.scalar.activation(out=ws[i][:], in_=ws[i][:], func=ACT.Square, scale=sqs[:, 0:1])
+            for s in pieces(i):
+                nc.scalar.activation(out=ws[i][:, s], in_=ws[i][:, s], func=ACT.Square, scale=sqs[:, 0:1])
 
         def v3(i):
             n, mt = divmod(i, MT)
             cols = slice(n * CH, (n + 1) * CH)
-            if i >= G3_FROM and mt < MT - 1:
+            if i >= G3_FROM and mt < MT - 1 and i < NT - 2:
                 lo = n * CH - (G3_FROM // MT) * CH
                 nc.gpsimd.tensor_tensor(out=ws[i][:], in0=ws[i][:], in1=bprime[:, lo:lo + CH], op=ALU.add)
+                nc.sync.dma_start(out=of[mt * P:(mt + 1) * P, cols], in_=ws[i][:])
             else:
-                nc.vector.scalar_tensor_tensor(out=ws[i][:], in0=bias_ps[:, n % 2, :], scalar=sfac[:, 0:1],
-                                               in1=ws[i][:], op0=ALU.mult, op1=ALU.add)
-            nc.sync.dma_start(out=of[mt * P:(mt + 1) * P, cols], in_=ws[i][:])
+                for s in pieces(i):
+                    nc.vector.scalar_tensor_tensor(out=ws[i][:, s], in0=bias_ps[:, n % 2, s], scalar=sfac[:, 0:1],
+                                                   in1=ws[i][:, s], op0=ALU.mult, op1=ALU.add)
+                    nc.sync.dma_start(out=of[mt * P:(mt + 1) * P, n * CH + s.start:n * CH + s.stop],
+                                      in_=ws[i][:, s])
 
         def x_transposes(half):
             for c in range(PASSES):
@@ -280,7 +292,7 @@ def tile_yatnmn_kernel(tc, x, kernel, bias, alpha, out):
                     nc.vector.tensor_copy(out=dst, in_=src)
 
         def x_square(mt):
-            nc.scalar.activation(out=junk[:], in_=x_sb[:, mt, :], func=ACT.Square,
+            nc.scalar.activation(out=junk[:, 2 + mt % 2, :], in_=x_sb[:, mt, :], func=ACT.Square,
                                  accum_out=xs_raw[:, mt:mt + 1])
 
         al = const.tile([P, 1], BF16)
@@ -309,8 +321,8 @@ def tile_yatnmn_kernel(tc, x, kernel, bias, alpha, out):
         bprime = const.tile([P, O - (G3_FROM // MT) * CH], F32)
         warm = const.tile([P, 1], F32)
         nc.scalar.activation(out=warm[:], in_=sfac[:], func=ACT.Abs_reciprocal_sqrt)
-        junk = const.tile([P, D], BF16)
-        junkf = const.tile([P, P], F32)
+        junk = const.tile([P, 4, D], BF16)
+        junkf = const.tile([P, 2, P], F32)
         xs_raw = const.tile([P, MT], F32)
         xhalf = const.tile([P, MT], F32)
         xw = x_sb[:].bitcast(F32).rearrange("p m (c q u) -> p m c q u", c=PASSES, q=P, u=2)

@@ -32,7 +32,8 @@ LN_C0 = 2.0404600064606253
 FLOPS = 2 * T * D * O
 
 GRAM = [2,1,2,1,2,1,1,2]
-QS = 8
+QS = 16
+QS_FULL = 0
 QS_FROM = 6
 QG = 72
 QG_X = 96
@@ -103,7 +104,10 @@ def tile_yatnmn_kernel(tc, x, kernel, bias, alpha, out):
             return dst, src
 
         def s_groups(r):
-            return QS if r >= QS_FROM else 0
+            if r < QS_FROM:
+                return 0
+            n = (r - LR + LS) // MT
+            return QS_FULL if n < NCH and GRAM[n] == 1 else QS
 
         def g_groups(r):
             if r - LR - 1 in XC_STEPS:

@@ -35,7 +35,7 @@ GRAM = [2,1,2,1,2,1,1,2]
 QS = 16
 QS_FULL = 0
 QS_FROM = 6
-QG = 72
+QG = 80
 QG_X = 96
 X_STEPS = (-6, -4)
 XC_STEPS = (-5, -3)

from contextlib import ExitStack

import concourse.mybir as mybir
from concourse.masks import make_identity

F32 = mybir.dt.float32
BF16 = mybir.dt.bfloat16
U32 = mybir.dt.uint32
U8 = mybir.dt.uint8
FP8X4 = mybir.dt.float8_e4m3fn_x4
ALU = mybir.AluOpType
ACT = mybir.ActivationFunctionType
AX = mybir.AxisListType

P = 128
D = 2048
O = 4096
T = 512
MT = T // P
PACK = 4
K_PASS = P * PACK
PASSES = D // K_PASS
CH = 512
NCH = O // CH
NT = NCH * MT
BLK = 128
NBLK = CH // BLK
ROWS = PASSES * PACK
EPS = 1.0 / 137.0
LN_C0 = 2.0404600064606253

FLOPS = 2 * T * D * O

GRAM = [2,1,2,1,2,1,1,2]
QS = 16
QS_FULL = 0
QS_FROM = 6
QG = 80
QG_X = 96
X_STEPS = (-6, -4)
XC_STEPS = (-5, -3)
QG_FROM = 7
X_EVAC_S = []
G3_FROM = 24
LR = 7
LS = 6
LMX = 2
MANUAL = True


def tile_yatnmn_kernel(tc, x, kernel, bias, alpha, out):
    nc = tc.nc
    xf = x.flatten_outer_dims()
    of = out.flatten_outer_dims()

    with ExitStack() as ctx:
        if MANUAL:
            ctx.enter_context(tc.manual_schedule())
        const = ctx.enter_context(tc.tile_pool(name="const", bufs=1))
        rawp = ctx.enter_context(tc.tile_pool(name="rawp", bufs=4))
        grp = ctx.enter_context(tc.tile_pool(name="grp", bufs=2))
        codep = ctx.enter_context(tc.tile_pool(name="codep", bufs=3))
        smallp = ctx.enter_context(tc.tile_pool(name="smallp", bufs=3))
        workp = ctx.enter_context(tc.tile_pool(name="workp", bufs=6))
        psy = ctx.enter_context(tc.psum_pool(name="psy", bufs=4))
        pstr = ctx.enter_context(tc.psum_pool(name="pstr", bufs=2))
        psk = ctx.enter_context(tc.psum_pool(name="psk", bufs=1))
        psbias = ctx.enter_context(tc.psum_pool(name="psbias", bufs=1))

        ident_b = const.tile([P, P], BF16)
        make_identity(nc, ident_b[:])
        ident_f = const.tile([P, P], F32)
        make_identity(nc, ident_f[:])

        raws = {}
        gks = {}
        codes = {}
        trs = {}
        parts = {}
        ksqs = {}
        grams = {}
        bcs = {}
        cbs = {}
        ys = {}
        ws = {}
        xts = {}

        def load_pass(n, c):
            nc.sync.dma_start(
                out=raws[n][:, c, :, :],
                in_=kernel[c * K_PASS:(c + 1) * K_PASS, n * CH:(n + 1) * CH].rearrange(
                    "(p j) w -> p j w", j=PACK))

        def load(n):
            raw = rawp.tile([P, PASSES, PACK, CH], BF16, tag="raw")
            raws[n] = raw
            for c in range(PASSES):
                load_pass(n, c)

        def views(r):
            n, c = divmod(r, PASSES)
            dst = gks[r][:].rearrange("p (q i t) -> p q t i", i=4, t=PACK)
            src = raws[n][:, c, :, :].rearrange("p t (q i) -> p q t i", i=4)
            return dst, src

        def s_groups(r):
            if r < QS_FROM:
                return 0
            n = (r - LR + LS) // MT
            return QS_FULL if n < NCH and GRAM[n] == 1 else QS

        def g_groups(r):
            if r - LR - 1 in XC_STEPS:
                return QG_X
            return QG if r >= QG_FROM else 0

        def regroup_g(r):
            gk = grp.tile([P, PACK * CH], BF16, tag="gk", align_bytes=64)
            gks[r] = gk
            n, c = divmod(r, PASSES)
            c0 = CH - 4 * g_groups(r)
            if c0 < CH:
                nc.gpsimd.tensor_scalar(
                    out=gk[:, PACK * c0:PACK * CH].rearrange("p (w t) -> p w t", t=PACK),
                    in0=raws[n][:, c, :, c0:CH].rearrange("p t w -> p w t"),
                    scalar1=1.0, scalar2=0.0, op0=ALU.mult, op1=ALU.add)

        def regroup_v(r):
            dst, src = views(r)
            qv = CH // 4 - s_groups(r) - g_groups(r)
            nc.vector.tensor_copy(out=dst[:, 0:qv], in_=src[:, 0:qv])

        def regroup_s(r):
            dst, src = views(r)
            qv = CH // 4 - s_groups(r) - g_groups(r)
            qe = CH // 4 - g_groups(r)
            if qv < qe:
                nc.scalar.copy(out=dst[:, qv:qe], in_=src[:, qv:qe])

        def quantise(r):
            n, c = divmod(r, PASSES)
            if c == 0:
                kc = codep.tile([P, PASSES, CH], U32, align_bytes=64)
                ksc = codep.tile([P, PASSES, CH], U8, align_bytes=64)
                codes[n] = (kc, ksc)
            kc, ksc = codes[n]
            nc.vector.quantize_mx(out=kc[:, c, :].bitcast(FP8X4), scales=ksc[:, c, :], in_=gks[r][:])

        def banks(n):
            return [(b, h) for h in range(2) for b in range(GRAM[n], NBLK)]

        def bank_step(n, k):
            if n == 0:
                return -LS + k // 2
            return MT * n - LS + (k * MT) // len(banks(n))

        def sum_step(n):
            return MT * n - 2 if n else -3

        def copy_step(n):
            return MT * n - 1 if n else -2

        def gram_step(n):
            return MT * n - 4 if n else -5

        def transposes(n, k):
            b, h = banks(n)[k]
            tr = pstr.tile([P, 8 * P], BF16)
            trs[(n, k)] = tr
            for i in range(8):
                c, j = divmod(h * 8 + i, PACK)
                nc.tensor.transpose(out=tr[:, i * P:(i + 1) * P],
                                    in_=raws[n][:, c, j, b * BLK:(b + 1) * BLK],
                                    identity=ident_b[:])

        def squares(n, k):
            b, h = banks(n)[k]
            if k == 0:
                part = smallp.tile([P, 2 * NBLK], F32)
                parts[n] = part
            idx = b * 2 + h
            nc.scalar.activation(out=junk[:, k % 2, 0:8 * P], in_=trs[(n, k)][:], func=ACT.Square,
                                 accum_out=parts[n][:, idx:idx + 1])

        def gram_blocks(n):
            gram = psk.tile([P, NBLK, P], F32, tag="k")
            grams[n] = gram
            for b in range(GRAM[n]):
                for r in range(ROWS):
                    c, j = divmod(r, PACK)
                    nc.tensor.matmul(out=gram[:, b, :], lhsT=raws[n][:, c, j, b * BLK:(b + 1) * BLK],
                                     rhs=raws[n][:, c, j, b * BLK:(b + 1) * BLK],
                                     start=(r == 0), stop=(r == ROWS - 1))

        def ksq_final(n):
            ng = GRAM[n]
            ksq = smallp.tile([P, NBLK], F32)
            ksqs[n] = ksq
            for b in range(ng):
                nc.vector.scalar_tensor_tensor(out=junkf[:, b, :], in0=grams[n][:, b, :], scalar=1.0,
                                               in1=ident_f[:], op0=ALU.mult, op1=ALU.mult,
                                               accum_out=ksq[:, b:b + 1])
            nc.vector.tensor_reduce(out=ksq[:, ng:NBLK],
                                    in_=parts[n][:, 2 * ng:2 * NBLK].rearrange("p (b h) -> p b h", h=2),
                                    axis=AX.X, op=ALU.add)

        def spread(n):
            bc = psk.tile([P, CH], F32, tag="k")
            bcs[n] = bc
            for b in range(NBLK):
                nc.tensor.transpose(out=bc[:, b * BLK:(b + 1) * BLK],
                                    in_=ksqs[n][:, b:b + 1].to_broadcast([P, P]),
                                    identity=ident_f[:])

        def cb_copy(n):
            cb = smallp.tile([P, CH], F32)
            cbs[n] = cb
            nc.scalar.activation(out=cb[:], in_=bcs[n][:], func=ACT.Copy, scale=0.5, bias=0.5 * EPS)

        def bias_spread(n):
            for b in range(NBLK):
                nc.tensor.transpose(out=bias_ps[:, n % 2, b * BLK:(b + 1) * BLK],
                                    in_=bias_t[:, NBLK * n + b:NBLK * n + b + 1].to_broadcast([P, P]),
                                    identity=ident_b[:])

        def mx(i):
            n, mt = divmod(i, MT)
            kc, ksc = codes[n]
            y = psy.tile([P, CH], F32, tag="y")
            ys[i] = y
            for c in range(PASSES):
                nc.tensor.matmul_mx(
                    out=y[:],
                    lhsT=xc[:, c, mt * P:(mt + 1) * P].bitcast(FP8X4),
                    lhsT_scale=xsc[:, c, mt * P:(mt + 1) * P],
                    rhs=kc[:, c, :].bitcast(FP8X4),
                    rhs_scale=ksc[:, c, :],
                    start=(c == 0), stop=(c == PASSES - 1))

        def pieces(i):
            if i == NT - 1:
                return [slice(0, CH // 2), slice(CH // 2, CH)]
            return [slice(0, CH)]

        def v1(i):
            n, mt = divmod(i, MT)
            w = workp.tile([P, CH], F32)
            ws[i] = w
            for s in pieces(i):
                nc.vector.scalar_tensor_tensor(out=w[:, s], in0=ys[i][:, s], scalar=xhalf[:, mt:mt + 1],
                                               in1=cbs[n][:, s], op0=ALU.subtract, op1=ALU.subtract)

        def s1(i):
            for s in pieces(i):
                nc.scalar.activation(out=ws[i][:, s], in_=ws[i][:, s], func=ACT.Abs_reciprocal_sqrt, scale=2.0)

        def v2(i):
            for s in pieces(i):
                nc.vector.tensor_tensor(out=ws[i][:, s], in0=ys[i][:, s], in1=ws[i][:, s], op=ALU.mult)

        def s2(i):
            for s in pieces(i):
                nc.scalar.activation(out=ws[i][:, s], in_=ws[i][:, s], func=ACT.Square, scale=sqs[:, 0:1])

        def v3(i):
            n, mt = divmod(i, MT)
            cols = slice(n * CH, (n + 1) * CH)
            if i >= G3_FROM and mt < MT - 1 and i < NT - 2:
                lo = n * CH - (G3_FROM // MT) * CH
                nc.gpsimd.tensor_tensor(out=ws[i][:], in0=ws[i][:], in1=bprime[:, lo:lo + CH], op=ALU.add)
                nc.sync.dma_start(out=of[mt * P:(mt + 1) * P, cols], in_=ws[i][:])
            else:
                for s in pieces(i):
                    nc.vector.scalar_tensor_tensor(out=ws[i][:, s], in0=bias_ps[:, n % 2, s], scalar=sfac[:, 0:1],
                                                   in1=ws[i][:, s], op0=ALU.mult, op1=ALU.add)
                    nc.sync.dma_start(out=of[mt * P:(mt + 1) * P, n * CH + s.start:n * CH + s.stop],
                                      in_=ws[i][:, s])

        def x_transposes(half):
            for c in range(PASSES):
                xt = psy.tile([P, 2, 2 * P], F32, tag="y")
                xts[(c, half)] = xt
                for u in range(2):
                    for ml in range(2):
                        nc.tensor.transpose(out=xt[:, u, ml * P:(ml + 1) * P],
                                            in_=xw[:, 2 * half + ml, c, :, u],
                                            identity=ident_f[:])

        def x_copies(half):
            for c in range(PASSES):
                dst = gx32[:, c, half * 2 * P:(half + 1) * 2 * P, :]
                src = xts[(c, half)][:].rearrange("p u t -> p t u")
                if c in X_EVAC_S:
                    nc.scalar.copy(out=dst, in_=src)
                else:
                    nc.vector.tensor_copy(out=dst, in_=src)

        def x_square(mt):
            nc.scalar.activation(out=junk[:, 2 + mt % 2, :], in_=x_sb[:, mt, :], func=ACT.Square,
                                 accum_out=xs_raw[:, mt:mt + 1])

        al = const.tile([P, 1], BF16)
        nc.scalar.dma_start(out=al[:], in_=alpha.partition_broadcast(P))
        raw0 = rawp.tile([P, PASSES, PACK, CH], BF16, tag="raw")
        raws[0] = raw0
        x_sb = rawp.tile([P, MT, D], BF16, tag="raw")
        bias_rows = const.tile([P, P], BF16)
        nc.gpsimd.memset(bias_rows[:], 0.0)
        for i in range(MT):
            load_pass(0, i)
            nc.sync.dma_start(out=x_sb[:, i, :], in_=xf[i * P:(i + 1) * P, :])
            if i == 0:
                nc.sync.dma_start(out=bias_rows[0:O // P, :], in_=bias.rearrange("(j q) -> j q", q=P))
        load(1)
        load(2)
        bias_b = const.tile([P, O - (G3_FROM // MT) * CH], BF16)
        nc.sync.dma_start(out=bias_b[:], in_=bias[(G3_FROM // MT) * CH:O].partition_broadcast(P))
        bias_ps = psbias.tile([P, 2, CH], BF16)
        bias_t = const.tile([P, O // P], BF16)

        sqs = const.tile([P, 1], F32)
        nc.scalar.activation(out=sqs[:], in_=al[:], func=ACT.Exp, scale=0.5 * LN_C0)
        sfac = const.tile([P, 1], F32)
        nc.scalar.activation(out=sfac[:], in_=al[:], func=ACT.Exp, scale=LN_C0)
        bprime = const.tile([P, O - (G3_FROM // MT) * CH], F32)
        warm = const.tile([P, 1], F32)
        nc.scalar.activation(out=warm[:], in_=sfac[:], func=ACT.Abs_reciprocal_sqrt)
        junk = const.tile([P, 4, D], BF16)
        junkf = const.tile([P, 2, P], F32)
        xs_raw = const.tile([P, MT], F32)
        xhalf = const.tile([P, MT], F32)
        xw = x_sb[:].bitcast(F32).rearrange("p m (c q u) -> p m c q u", c=PASSES, q=P, u=2)
        gx = const.tile([P, PASSES, PACK * T], BF16, align_bytes=64)
        gx32 = gx[:].bitcast(F32).rearrange("p c (t u) -> p c t u", u=2)
        xc = const.tile([P, PASSES, T], U32, align_bytes=64)
        xsc = const.tile([P, PASSES, T], U8, align_bytes=64)

        first = -max(LR, LS + 1)
        for i in range(first, NT + 2):
            if (i + 15) % MT == 0 and 3 <= (i + 15) // MT < NCH:
                load((i + 15) // MT)
            if 0 <= i + LMX < NT:
                mx(i + LMX)
            r = i + LR
            if 0 <= r < NCH * PASSES:
                regroup_g(r)
            if i == G3_FROM + 1:
                nc.gpsimd.tensor_scalar(out=bprime[:], in0=bias_b[:], scalar1=sfac[:, 0:1],
                                        scalar2=0.0, op0=ALU.mult, op1=ALU.add)
            if 0 <= i < NT:
                v1(i)
            if 0 <= i - 1 < NT:
                v2(i - 1)
            for n in range(NCH):
                if copy_step(n) == i:
                    cb_copy(n)
            if 0 <= i < NT:
                s1(i)
            if 0 <= i - 1 < NT:
                s2(i - 1)
            if i == -1:
                nc.vector.tensor_scalar(out=xhalf[:], in0=xs_raw[:], scalar1=0.5, scalar2=None,
                                        op0=ALU.mult)
            if 0 <= i - 2 < NT:
                v3(i - 2)
            if 0 <= r - 1 < NCH * PASSES:
                quantise(r - 1)
            if 0 <= r < NCH * PASSES:
                regroup_v(r)
            for n in range(NCH):
                if sum_step(n) == i:
                    ksq_final(n)
            if i == -4:
                nc.vector.tensor_copy(out=bias_t[:], in_=bias_ps[:, 1, 0:O // P])
            if i in X_STEPS:
                x_transposes(X_STEPS.index(i))
            if i in XC_STEPS:
                x_copies(XC_STEPS.index(i))
            if i == -3:
                for c in range(PASSES):
                    nc.vector.quantize_mx(out=xc[:, c, :].bitcast(FP8X4), scales=xsc[:, c, :],
                                          in_=gx[:, c, :])
            if 0 <= r < NCH * PASSES:
                regroup_s(r)
            for n in range(NCH):
                for k in range(len(banks(n))):
                    if bank_step(n, k) == i:
                        squares(n, k)
            if -7 <= i <= -4:
                x_square(i + 7)
            if i == -6:
                nc.tensor.transpose(out=bias_ps[:, 1, 0:P], in_=bias_rows[:], identity=ident_b[:])
            for n in range(NCH):
                if sum_step(n) == i:
                    spread(n)
                    bias_spread(n)
            for n in range(NCH):
                for k in range(len(banks(n))):
                    if bank_step(n, k) == i + 1:
                        transposes(n, k)
            for n in range(NCH):
                if gram_step(n) == i:
                    gram_blocks(n)
